import numpy as np
import ml_dtypes


def mxq(x, axis, fmt="e4m3"):
    dtype, down = {"e4m3": (ml_dtypes.float8_e4m3fn, 7), "e5m2": (ml_dtypes.float8_e5m2, 14)}[fmt]
    v = np.moveaxis(np.asarray(x, np.float32).astype(ml_dtypes.bfloat16).astype(np.float64), axis, -1)
    blocks = v.reshape(v.shape[:-1] + (-1, 32))
    amax = np.abs(blocks).max(-1, keepdims=True)
    byte = np.maximum(np.where(amax > 0, np.frexp(amax)[1] - 1 + 127, 0) - down, 1)
    scale = np.exp2(byte - 127.0)
    codes = (blocks / scale).astype(np.float32).astype(dtype).astype(np.float64)
    return np.moveaxis((codes * scale).reshape(v.shape), -1, axis)


WIDE = False


def mx_kscale(k):
    if not WIDE:
        return np.ones(k)
    levels = np.array([10, -10, 5, -5, 0])
    a = np.random.permutation(np.resize(levels, k // 512 * 4)).reshape(k // 512, 4)
    idx = np.arange(k)
    return np.exp2(a[idx // 512, idx % 128 // 32])


BF16 = ml_dtypes.bfloat16


def bf(x):
    return np.asarray(x, np.float32).astype(BF16)


def f64(x):
    return np.asarray(x).astype(np.float64)


B, S, NI, NO = 4, 576, 128, 128


def setup_inputs():
    sn = mx_kscale(4 * NI)[::4]
    sc = NI ** -0.5

    def u():
        return bf(np.random.uniform(-sc, sc, (NO, NI)) / sn[None, :])

    return {"q_in": bf(np.random.standard_normal((B, S, 4 * NI)) * np.repeat(sn, 4)),
            "r_weight": u(), "i_weight": u(), "j_weight": u(), "k_weight": u()}


def reference(q_in, r_weight, i_weight, j_weight, k_weight):
    q = f64(q_in)
    V = np.stack([f64(r_weight), f64(i_weight), f64(j_weight), f64(k_weight)]).transpose(2, 0, 1).reshape(4 * NI, NO)
    Vq = mxq(V, 0, "e4m3")
    Wr, Wi, Wj, Wk = Vq.reshape(NI, 4, NO).transpose(1, 2, 0)
    W4 = np.stack([
        np.stack([Wr, -Wi, -Wj, -Wk]),
        np.stack([Wi, Wr, Wk, -Wj]),
        np.stack([Wj, -Wk, Wr, Wi]),
        np.stack([Wk, Wj, -Wi, Wr]),
    ])
    W = W4.transpose(3, 1, 2, 0).reshape(4 * NI, 4 * NO)
    return mxq(q, 2, "e4m3") @ W

@@ -1,0 +1,143 @@
+from contextlib import ExitStack
+
+import concourse.mybir as mybir
+from concourse.masks import make_identity
+
+F32 = mybir.dt.float32
+BF16 = mybir.dt.bfloat16
+U32 = mybir.dt.uint32
+U8 = mybir.dt.uint8
+FP8X4 = mybir.dt.float8_e4m3fn_x4
+
+P = 128
+TOKENS = 4 * 576
+K = 512
+N_OUT = 512
+TILES = TOKENS // P
+PAIRS = TILES // 2
+FLOPS = 2 * TOKENS * K * N_OUT
+
+LOAD_CHUNKS = (2, 4, 6, 6)
+E_ENGINE = "SSSVVVVVV"
+O_ENGINE = "SSSSSSSSSSSVSVSVSV"
+R_ENGINE = "VVSS"
+PINNED = False
+
+
+def tile_quaternionlinear_kernel(tc, q_in, r_weight, i_weight, j_weight, k_weight, out):
+    nc = tc.nc
+    q_view = q_in.flatten_outer_dims().rearrange("(p t) k -> p t k", t=TILES)
+    out_view = out.flatten_outer_dims().rearrange("(p t) c -> p t c", t=TILES)
+
+    def copy(engine, dst, src):
+        if engine == "V":
+            nc.vector.tensor_copy(out=dst, in_=src)
+        else:
+            nc.scalar.copy(out=dst, in_=src)
+
+    with ExitStack() as ctx:
+        keep = ctx.enter_context(tc.tile_pool(name="keep", bufs=1))
+        psum_t = ctx.enter_context(tc.psum_pool(name="psum_t", bufs=3))
+        psum_o = ctx.enter_context(tc.psum_pool(name="psum_o", bufs=5))
+        if PINNED:
+            ctx.enter_context(tc.manual_schedule())
+
+        planes = keep.tile([P, 9, P], BF16, name="planes")
+        nc.sync.dma_start(out=planes[:, 0:9:8, :], in_=i_weight.unsqueeze(1).to_broadcast([P, 2, P]))
+        nc.sync.dma_start(out=planes[:, 1:8:6, :], in_=r_weight.unsqueeze(1).to_broadcast([P, 2, P]))
+        nc.sync.dma_start(out=planes[:, 2, :], in_=k_weight)
+        nc.sync.dma_start(out=planes[:, 5, :], in_=j_weight)
+
+        q_tiles = []
+        first = 0
+        for ci, n in enumerate(LOAD_CHUNKS):
+            q_chunk = keep.tile([P, n, K], BF16, name="q_chunk%d" % ci)
+            nc.sync.dma_start(out=q_chunk[:], in_=q_view[:, first : first + n, :])
+            for j in range(n):
+                q_tiles.append(q_chunk[:, j, :])
+            first += n
+
+        ident = keep.tile([P, P], F32, name="ident")
+        make_identity(nc, ident[:])
+
+        nc.vector.tensor_scalar_mul(out=planes[:, 4:7:2, :], in0=planes[:, 0:3:2, :], scalar1=-1.0)
+        nc.vector.tensor_scalar_mul(out=planes[:, 3, :], in0=planes[:, 5, :], scalar1=-1.0)
+
+        signed = keep.tile([P, 4, P, 4], BF16, name="signed")
+
+        def plane_grid(d):
+            if d == 1:
+                return planes[:, 0:4, :].rearrange("p (b e) n -> p n b e", e=2)
+            if d == 2:
+                return planes[:, 5:9, :].rearrange("p (b e) n -> p n b e", e=2)
+            base = 1 if d == 0 else 2
+            six = planes[:, base : base + 6, :].rearrange("p (e x) n -> p e x n", x=3)
+            return six[:, :, 0:3:2, :].rearrange("p e b n -> p n b e")
+
+        for d in (1, 0, 2, 3):
+            copy(R_ENGINE[d], signed[:, d, :, :].rearrange("p n (b e) -> p n b e", e=2), plane_grid(d))
+
+        signed_words = signed[:].rearrange("p d n c -> p (d n c)").bitcast(F32)
+        w_grouped = keep.tile([P, 4 * N_OUT], BF16, name="w_grouped", align_bytes=64)
+        w_grouped_words = w_grouped[:].bitcast(F32).rearrange("p (m x) -> p m x", x=8)
+        w_codes = keep.tile([P, N_OUT], U32, name="w_codes", align_bytes=64)
+        w_scales = keep.tile([P, N_OUT], U8, name="w_scales", align_bytes=64)
+
+        def weights_to_codes():
+            for h in range(2):
+                tw = psum_t.tile([P, 4, P], F32, tag="t", name="tw%d" % h)
+                for x in range(4):
+                    col = (4 * h + x) * P
+                    nc.tensor.transpose(tw[:, x, :], signed_words[:, col : col + P], ident[:])
+                copy("V", w_grouped_words[:, :, 4 * h : 4 * h + 4], tw[:].rearrange("p x m -> p m x"))
+            nc.vector.quantize_mx(out=w_codes[:].bitcast(FP8X4), scales=w_scales[:], in_=w_grouped[:])
+
+        q_codes = []
+        q_scales = []
+
+        def prepare(i):
+            tq = psum_t.tile([P, 2, 2, P], F32, tag="t", name="tq%d" % i)
+            for s in range(2):
+                words = q_tiles[2 * i + s].bitcast(F32)
+                for u in range(2):
+                    nc.tensor.transpose(tq[:, s, u, :], words[:, u * P : (u + 1) * P], ident[:])
+            grouped = keep.tile([P, 8 * P], BF16, name="grouped%d" % i, align_bytes=64)
+            copy(
+                E_ENGINE[i],
+                grouped[:].bitcast(F32).rearrange("p (s k u) -> p s k u", s=2, u=2),
+                tq[:].rearrange("p s u k -> p s k u"),
+            )
+            codes = keep.tile([P, 2 * P], U32, name="codes%d" % i, align_bytes=64)
+            scales = keep.tile([P, 2 * P], U8, name="scales%d" % i, align_bytes=64)
+            nc.vector.quantize_mx(out=codes[:].bitcast(FP8X4), scales=scales[:], in_=grouped[:])
+            q_codes.append(codes)
+            q_scales.append(scales)
+
+        def multiply(i):
+            o_sb = keep.tile([P, 2, N_OUT], F32, name="o_sb%d" % i)
+            for s in range(2):
+                acc = psum_o.tile([P, N_OUT], F32, tag="o", name="acc%d_%d" % (i, s))
+                nc.tensor.matmul_mx(
+                    out=acc[:],
+                    lhsT=q_codes[i][:, s * P : (s + 1) * P].bitcast(FP8X4),
+                    lhsT_scale=q_scales[i][:, s * P : (s + 1) * P],
+                    rhs=w_codes[:].bitcast(FP8X4),
+                    rhs_scale=w_scales[:],
+                    start=True,
+                    stop=True,
+                )
+                copy(O_ENGINE[2 * i + s], o_sb[:, s, :], acc[:])
+            nc.sync.dma_start(out=out_view[:, 2 * i : 2 * i + 2, :], in_=o_sb[:])
+
+        prepare(0)
+        weights_to_codes()
+        prepare(1)
+        prepare(2)
+        for i in range(3, PAIRS, 2):
+            multiply(i - 3)
+            multiply(i - 2)
+            prepare(i)
+            prepare(i + 1)
+        multiply(PAIRS - 3)
+        multiply(PAIRS - 2)
+        multiply(PAIRS - 1)

@@ -8,20 +8,24 @@ BF16 = mybir.dt.bfloat16
 U32 = mybir.dt.uint32
 U8 = mybir.dt.uint8
 FP8X4 = mybir.dt.float8_e4m3fn_x4
+MULT = mybir.AluOpType.mult
+ADD = mybir.AluOpType.add
 
 P = 128
 TOKENS = 4 * 576
 K = 512
 N_OUT = 512
 TILES = TOKENS // P
-PAIRS = TILES // 2
 FLOPS = 2 * TOKENS * K * N_OUT
 
-LOAD_CHUNKS = (2, 4, 6, 6)
-E_ENGINE = "SSSVVVVVV"
-O_ENGINE = "SSSSSSSSSSSVSVSVSV"
-R_ENGINE = "VVSS"
-PINNED = False
+LOAD_CHUNKS = (1, 3, 6, 8)
+GROUPS = ((0,), (1,), (2, 3), (4, 5), (6, 7), (8, 9), (10, 11), (12, 13), (14, 15), (16, 17))
+STORES = ((0,), (1,), (2, 3), (4, 5), (6, 7), (8, 9), (10, 11), (12, 13), (14, 15), (16,), (17,))
+E_ENGINE = "SSSVVVVVVV"
+O_ENGINE = "SSSSSSSSSSSSSVSVSV"
+R_ENGINE = "VSVV"
+TAIL = ("p2", "MA", "m1", "p3", "m2", "p4", "p5", "m3", "p6", "m4", "p7", "m5", "p8", "m6", "p9", "m7", "m8", "m9")
+PINNED = True
 
 
 def tile_quaternionlinear_kernel(tc, q_in, r_weight, i_weight, j_weight, k_weight, out):
@@ -44,9 +48,9 @@ def tile_quaternionlinear_kernel(tc, q_in, r_weight, i_weight, j_weight, k_weigh
 
         planes = keep.tile([P, 9, P], BF16, name="planes")
         nc.sync.dma_start(out=planes[:, 0:9:8, :], in_=i_weight.unsqueeze(1).to_broadcast([P, 2, P]))
-        nc.sync.dma_start(out=planes[:, 1:8:6, :], in_=r_weight.unsqueeze(1).to_broadcast([P, 2, P]))
         nc.sync.dma_start(out=planes[:, 2, :], in_=k_weight)
         nc.sync.dma_start(out=planes[:, 5, :], in_=j_weight)
+        nc.sync.dma_start(out=planes[:, 1:8:6, :], in_=r_weight.unsqueeze(1).to_broadcast([P, 2, P]))
 
         q_tiles = []
         first = 0
@@ -60,10 +64,12 @@ def tile_quaternionlinear_kernel(tc, q_in, r_weight, i_weight, j_weight, k_weigh
         ident = keep.tile([P, P], F32, name="ident")
         make_identity(nc, ident[:])
 
-        nc.vector.tensor_scalar_mul(out=planes[:, 4:7:2, :], in0=planes[:, 0:3:2, :], scalar1=-1.0)
-        nc.vector.tensor_scalar_mul(out=planes[:, 3, :], in0=planes[:, 5, :], scalar1=-1.0)
-
         signed = keep.tile([P, 4, P, 4], BF16, name="signed")
+        signed_words = signed[:].rearrange("p d n c -> p (d n c)").bitcast(F32)
+        w_codes = keep.tile([P, N_OUT], U32, name="w_codes", align_bytes=64)
+        w_scales = keep.tile([P, N_OUT], U8, name="w_scales", align_bytes=64)
+        w_banks = {}
+        w_grouped = {}
 
         def plane_grid(d):
             if d == 1:
@@ -74,70 +80,143 @@ def tile_quaternionlinear_kernel(tc, q_in, r_weight, i_weight, j_weight, k_weigh
             six = planes[:, base : base + 6, :].rearrange("p (e x) n -> p e x n", x=3)
             return six[:, :, 0:3:2, :].rearrange("p e b n -> p n b e")
 
-        for d in (1, 0, 2, 3):
+        def negate_ik():
+            nc.vector.tensor_scalar_mul(out=planes[:, 4:7:2, :], in0=planes[:, 0:3:2, :], scalar1=-1.0)
+
+        def negate_j():
+            nc.gpsimd.tensor_scalar(out=planes[:, 3, :], in0=planes[:, 5, :], scalar1=-1.0, scalar2=0.0, op0=MULT, op1=ADD)
+
+        def regroup(d):
             copy(R_ENGINE[d], signed[:, d, :, :].rearrange("p n (b e) -> p n b e", e=2), plane_grid(d))
 
-        signed_words = signed[:].rearrange("p d n c -> p (d n c)").bitcast(F32)
-        w_grouped = keep.tile([P, 4 * N_OUT], BF16, name="w_grouped", align_bytes=64)
-        w_grouped_words = w_grouped[:].bitcast(F32).rearrange("p (m x) -> p m x", x=8)
-        w_codes = keep.tile([P, N_OUT], U32, name="w_codes", align_bytes=64)
-        w_scales = keep.tile([P, N_OUT], U8, name="w_scales", align_bytes=64)
+        def w_transpose(d):
+            tw = psum_o.tile([P, 2, P], F32, tag="o", name="tw%d" % d)
+            for u in range(2):
+                col = (2 * d + u) * P
+                nc.tensor.transpose(tw[:, u, :], signed_words[:, col : col + P], ident[:])
+            w_banks[d] = tw
 
-        def weights_to_codes():
-            for h in range(2):
-                tw = psum_t.tile([P, 4, P], F32, tag="t", name="tw%d" % h)
-                for x in range(4):
-                    col = (4 * h + x) * P
-                    nc.tensor.transpose(tw[:, x, :], signed_words[:, col : col + P], ident[:])
-                copy("V", w_grouped_words[:, :, 4 * h : 4 * h + 4], tw[:].rearrange("p x m -> p m x"))
-            nc.vector.quantize_mx(out=w_codes[:].bitcast(FP8X4), scales=w_scales[:], in_=w_grouped[:])
+        def w_evacuate(d):
+            wg = keep.tile([P, 4 * P], BF16, name="w_grouped%d" % d, align_bytes=64)
+            copy("S", wg[:].bitcast(F32).rearrange("p (m u) -> p m u", u=2), w_banks[d][:].rearrange("p u m -> p m u"))
+            w_grouped[d] = wg
 
-        q_codes = []
-        q_scales = []
+        def w_quantise(d):
+            cols = slice(d * P, (d + 1) * P)
+            nc.vector.quantize_mx(out=w_codes[:, cols].bitcast(FP8X4), scales=w_scales[:, cols], in_=w_grouped[d][:])
 
-        def prepare(i):
-            tq = psum_t.tile([P, 2, 2, P], F32, tag="t", name="tq%d" % i)
-            for s in range(2):
-                words = q_tiles[2 * i + s].bitcast(F32)
+        q_banks = {}
+        q_grouped = {}
+        q_codes = {}
+        q_scales = {}
+        slot_of = {}
+        for g, tiles in enumerate(GROUPS):
+            for s, t in enumerate(tiles):
+                slot_of[t] = (g, s)
+
+        def q_transpose(g):
+            n = len(GROUPS[g])
+            tq = psum_t.tile([P, n, 2, P], F32, tag="t", name="tq%d" % g)
+            for s, t in enumerate(GROUPS[g]):
+                words = q_tiles[t].bitcast(F32)
                 for u in range(2):
                     nc.tensor.transpose(tq[:, s, u, :], words[:, u * P : (u + 1) * P], ident[:])
-            grouped = keep.tile([P, 8 * P], BF16, name="grouped%d" % i, align_bytes=64)
-            copy(
-                E_ENGINE[i],
-                grouped[:].bitcast(F32).rearrange("p (s k u) -> p s k u", s=2, u=2),
-                tq[:].rearrange("p s u k -> p s k u"),
-            )
-            codes = keep.tile([P, 2 * P], U32, name="codes%d" % i, align_bytes=64)
-            scales = keep.tile([P, 2 * P], U8, name="scales%d" % i, align_bytes=64)
-            nc.vector.quantize_mx(out=codes[:].bitcast(FP8X4), scales=scales[:], in_=grouped[:])
-            q_codes.append(codes)
-            q_scales.append(scales)
+            q_banks[g] = tq
 
-        def multiply(i):
-            o_sb = keep.tile([P, 2, N_OUT], F32, name="o_sb%d" % i)
-            for s in range(2):
-                acc = psum_o.tile([P, N_OUT], F32, tag="o", name="acc%d_%d" % (i, s))
+        def q_evacuate(g):
+            n = len(GROUPS[g])
+            grouped = keep.tile([P, n * 4 * P], BF16, name="grouped%d" % g, align_bytes=64)
+            copy(
+                E_ENGINE[g],
+                grouped[:].bitcast(F32).rearrange("p (s k u) -> p s k u", s=n, u=2),
+                q_banks[g][:].rearrange("p s u k -> p s k u"),
+            )
+            q_grouped[g] = grouped
+
+        def q_quantise(g):
+            n = len(GROUPS[g])
+            codes = keep.tile([P, n * P], U32, name="codes%d" % g, align_bytes=64)
+            scales = keep.tile([P, n * P], U8, name="scales%d" % g, align_bytes=64)
+            nc.vector.quantize_mx(out=codes[:].bitcast(FP8X4), scales=scales[:], in_=q_grouped[g][:])
+            q_codes[g] = codes
+            q_scales[g] = scales
+
+        store_of = {}
+        o_tiles = {}
+        left = {}
+        for si, tiles in enumerate(STORES):
+            left[si] = len(tiles)
+            for s, t in enumerate(tiles):
+                store_of[t] = (si, s)
+
+        def multiply(t, by_component):
+            g, s = slot_of[t]
+            acc = psum_o.tile([P, N_OUT], F32, tag="o", name="acc%d" % t)
+            pieces = (3, 2, 1, 0) if by_component else (None,)
+            for d in pieces:
+                cols = slice(0, N_OUT) if d is None else slice(d * P, (d + 1) * P)
                 nc.tensor.matmul_mx(
-                    out=acc[:],
-                    lhsT=q_codes[i][:, s * P : (s + 1) * P].bitcast(FP8X4),
-                    lhsT_scale=q_scales[i][:, s * P : (s + 1) * P],
-                    rhs=w_codes[:].bitcast(FP8X4),
-                    rhs_scale=w_scales[:],
+                    out=acc[:, cols],
+                    lhsT=q_codes[g][:, s * P : (s + 1) * P].bitcast(FP8X4),
+                    lhsT_scale=q_scales[g][:, s * P : (s + 1) * P],
+                    rhs=w_codes[:, cols].bitcast(FP8X4),
+                    rhs_scale=w_scales[:, cols],
                     start=True,
                     stop=True,
                 )
-                copy(O_ENGINE[2 * i + s], o_sb[:, s, :], acc[:])
-            nc.sync.dma_start(out=out_view[:, 2 * i : 2 * i + 2, :], in_=o_sb[:])
+            si, ss = store_of[t]
+            if si not in o_tiles:
+                o_tiles[si] = keep.tile([P, len(STORES[si]), N_OUT], F32, name="o_sb%d" % si)
+            copy(
+                O_ENGINE[t],
+                o_tiles[si][:, ss, :].rearrange("p (m d) -> p m d", d=4),
+                acc[:].rearrange("p (d m) -> p m d", d=4),
+            )
+            left[si] -= 1
+            if left[si] == 0:
+                t0 = STORES[si][0]
+                nc.sync.dma_start(out=out_view[:, t0 : t0 + len(STORES[si]), :], in_=o_tiles[si][:])
 
-        prepare(0)
-        weights_to_codes()
-        prepare(1)
-        prepare(2)
-        for i in range(3, PAIRS, 2):
-            multiply(i - 3)
-            multiply(i - 2)
-            prepare(i)
-            prepare(i + 1)
-        multiply(PAIRS - 3)
-        multiply(PAIRS - 2)
-        multiply(PAIRS - 1)
+        negate_ik()
+        negate_j()
+        regroup(3)
+        regroup(1)
+        q_transpose(0)
+        regroup(2)
+        w_transpose(3)
+        q_evacuate(0)
+        regroup(0)
+        w_transpose(2)
+        w_evacuate(3)
+        q_quantise(0)
+        w_transpose(1)
+        w_evacuate(2)
+        w_quantise(3)
+        w_transpose(0)
+        w_evacuate(1)
+        w_quantise(2)
+        q_transpose(1)
+        w_evacuate(0)
+        w_quantise(1)
+        w_quantise(0)
+        q_evacuate(1)
+        q_quantise(1)
+
+        pending = []
+        for step in TAIL:
+            if step == "MA":
+                multiply(0, True)
+            elif step[0] == "p":
+                g = int(step[1:])
+                q_transpose(g)
+                q_evacuate(g)
+                for h in pending:
+                    q_quantise(h)
+                pending = [g]
+            else:
+                g = int(step[1:])
+                if g in pending:
+                    q_quantise(g)
+                    pending = []
+                for t in GROUPS[g]:
+                    multiply(t, False)

@@ -24,7 +24,21 @@ STORES = ((0,), (1,), (2, 3), (4, 5), (6, 7), (8, 9), (10, 11), (12, 13), (14, 1
 E_ENGINE = "SSSVVVVVVV"
 O_ENGINE = "SSSSSSSSSSSSSVSVSV"
 R_ENGINE = "VSVV"
-TAIL = ("p2", "MA", "m1", "p3", "m2", "p4", "p5", "m3", "p6", "m4", "p7", "m5", "p8", "m6", "p9", "m7", "m8", "m9")
+EW_ENGINE = "SSSS"
+ORDER = (
+    ("D", 5), ("NA", 0), ("NB", 0), ("R", 3), ("R", 1), ("T", 0), ("D", 1), ("R", 2),
+    ("TW", 3), ("D", 1), ("E", 0), ("R", 0), ("TW", 2), ("EW", 3), ("Q", 0), ("TW", 1),
+    ("D", 1), ("EW", 2), ("QW", 3), ("TW", 0), ("EW", 1), ("QW", 2), ("T", 1), ("EW", 0),
+    ("QW", 1), ("QW", 0), ("E", 1), ("Q", 1), ("T", 2), ("D", 1), ("E", 2), ("Q", 2),
+    ("MA", 3), ("MA", 2), ("MA", 1), ("MA", 0), ("O", 0), ("M", 1), ("O", 1), ("T", 3),
+    ("E", 3), ("Q", 3), ("M", 2), ("O", 2), ("M", 3), ("O", 3), ("T", 4), ("E", 4),
+    ("Q", 4), ("T", 5), ("E", 5), ("Q", 5), ("M", 4), ("O", 4), ("M", 5), ("O", 5),
+    ("T", 6), ("E", 6), ("Q", 6), ("M", 6), ("O", 6), ("M", 7), ("O", 7), ("T", 7),
+    ("E", 7), ("Q", 7), ("M", 8), ("O", 8), ("M", 9), ("O", 9), ("T", 8), ("E", 8),
+    ("Q", 8), ("M", 10), ("O", 10), ("M", 11), ("O", 11), ("T", 9), ("E", 9), ("Q", 9),
+    ("M", 12), ("O", 12), ("M", 13), ("O", 13), ("M", 14), ("O", 14), ("M", 15), ("O", 15),
+    ("M", 16), ("O", 16), ("M", 17), ("O", 17),
+)
 PINNED = True
 
 
@@ -41,7 +55,8 @@ def tile_quaternionlinear_kernel(tc, q_in, r_weight, i_weight, j_weight, k_weigh
 
     with ExitStack() as ctx:
         keep = ctx.enter_context(tc.tile_pool(name="keep", bufs=1))
-        psum_t = ctx.enter_context(tc.psum_pool(name="psum_t", bufs=3))
+        psum_t = ctx.enter_context(tc.psum_pool(name="psum_t", bufs=2))
+        psum_w = ctx.enter_context(tc.psum_pool(name="psum_w", bufs=1))
         psum_o = ctx.enter_context(tc.psum_pool(name="psum_o", bufs=5))
         if PINNED:
             ctx.enter_context(tc.manual_schedule())
@@ -98,7 +113,7 @@ def tile_quaternionlinear_kernel(tc, q_in, r_weight, i_weight, j_weight, k_weigh
 
         def w_evacuate(d):
             wg = keep.tile([P, 4 * P], BF16, name="w_grouped%d" % d, align_bytes=64)
-            copy("S", wg[:].bitcast(F32).rearrange("p (m u) -> p m u", u=2), w_banks[d][:].rearrange("p u m -> p m u"))
+            copy(EW_ENGINE[d], wg[:].bitcast(F32).rearrange("p (m u) -> p m u", u=2), w_banks[d][:].rearrange("p u m -> p m u"))
             w_grouped[d] = wg
 
         def w_quantise(d):
@@ -149,74 +164,71 @@ def tile_quaternionlinear_kernel(tc, q_in, r_weight, i_weight, j_weight, k_weigh
             for s, t in enumerate(tiles):
                 store_of[t] = (si, s)
 
-        def multiply(t, by_component):
+        accs = {}
+        warm_bank = psum_w.tile([P, P], F32, name="warm_bank")
+
+        def warm(n):
+            for r in range(n):
+                nc.tensor.matmul(out=warm_bank[:], lhsT=ident[:], rhs=ident[:], start=True, stop=True)
+
+
+        def multiply(t):
             g, s = slot_of[t]
             acc = psum_o.tile([P, N_OUT], F32, tag="o", name="acc%d" % t)
-            pieces = (3, 2, 1, 0) if by_component else (None,)
-            for d in pieces:
-                cols = slice(0, N_OUT) if d is None else slice(d * P, (d + 1) * P)
-                nc.tensor.matmul_mx(
-                    out=acc[:, cols],
-                    lhsT=q_codes[g][:, s * P : (s + 1) * P].bitcast(FP8X4),
-                    lhsT_scale=q_scales[g][:, s * P : (s + 1) * P],
-                    rhs=w_codes[:, cols].bitcast(FP8X4),
-                    rhs_scale=w_scales[:, cols],
-                    start=True,
-                    stop=True,
-                )
+            nc.tensor.matmul_mx(
+                out=acc[:],
+                lhsT=q_codes[g][:, s * P : (s + 1) * P].bitcast(FP8X4),
+                lhsT_scale=q_scales[g][:, s * P : (s + 1) * P],
+                rhs=w_codes[:].bitcast(FP8X4),
+                rhs_scale=w_scales[:],
+                start=True,
+                stop=True,
+            )
+            accs[t] = acc
+
+        def multiply_component(d):
+            g, s = slot_of[0]
+            if 0 not in accs:
+                accs[0] = psum_o.tile([P, N_OUT], F32, tag="o", name="acc0")
+            cols = slice(d * P, (d + 1) * P)
+            nc.tensor.matmul_mx(
+                out=accs[0][:, cols],
+                lhsT=q_codes[g][:, s * P : (s + 1) * P].bitcast(FP8X4),
+                lhsT_scale=q_scales[g][:, s * P : (s + 1) * P],
+                rhs=w_codes[:, cols].bitcast(FP8X4),
+                rhs_scale=w_scales[:, cols],
+                start=True,
+                stop=True,
+            )
+
+        def o_evacuate(t):
             si, ss = store_of[t]
             if si not in o_tiles:
                 o_tiles[si] = keep.tile([P, len(STORES[si]), N_OUT], F32, name="o_sb%d" % si)
             copy(
                 O_ENGINE[t],
                 o_tiles[si][:, ss, :].rearrange("p (m d) -> p m d", d=4),
-                acc[:].rearrange("p (d m) -> p m d", d=4),
+                accs[t][:].rearrange("p (d m) -> p m d", d=4),
             )
             left[si] -= 1
             if left[si] == 0:
                 t0 = STORES[si][0]
                 nc.sync.dma_start(out=out_view[:, t0 : t0 + len(STORES[si]), :], in_=o_tiles[si][:])
 
-        negate_ik()
-        negate_j()
-        regroup(3)
-        regroup(1)
-        q_transpose(0)
-        regroup(2)
-        w_transpose(3)
-        q_evacuate(0)
-        regroup(0)
-        w_transpose(2)
-        w_evacuate(3)
-        q_quantise(0)
-        w_transpose(1)
-        w_evacuate(2)
-        w_quantise(3)
-        w_transpose(0)
-        w_evacuate(1)
-        w_quantise(2)
-        q_transpose(1)
-        w_evacuate(0)
-        w_quantise(1)
-        w_quantise(0)
-        q_evacuate(1)
-        q_quantise(1)
-
-        pending = []
-        for step in TAIL:
-            if step == "MA":
-                multiply(0, True)
-            elif step[0] == "p":
-                g = int(step[1:])
-                q_transpose(g)
-                q_evacuate(g)
-                for h in pending:
-                    q_quantise(h)
-                pending = [g]
-            else:
-                g = int(step[1:])
-                if g in pending:
-                    q_quantise(g)
-                    pending = []
-                for t in GROUPS[g]:
-                    multiply(t, False)
+        actions = {
+            "NA": lambda x: negate_ik(),
+            "NB": lambda x: negate_j(),
+            "R": regroup,
+            "TW": w_transpose,
+            "EW": w_evacuate,
+            "QW": w_quantise,
+            "T": q_transpose,
+            "E": q_evacuate,
+            "Q": q_quantise,
+            "M": multiply,
+            "MA": multiply_component,
+            "O": o_evacuate,
+            "D": warm,
+        }
+        for name, index in ORDER:
+            actions[name](index)

@@ -18,21 +18,21 @@ N_OUT = 512
 TILES = TOKENS // P
 FLOPS = 2 * TOKENS * K * N_OUT
 
-LOAD_CHUNKS = (1, 3, 6, 8)
+LOAD_CHUNKS = (1, 3, 4, 4, 6)
 GROUPS = ((0,), (1,), (2, 3), (4, 5), (6, 7), (8, 9), (10, 11), (12, 13), (14, 15), (16, 17))
 STORES = ((0,), (1,), (2, 3), (4, 5), (6, 7), (8, 9), (10, 11), (12, 13), (14, 15), (16,), (17,))
 E_ENGINE = "SSSVVVVVVV"
 O_ENGINE = "SSSSSSSSSSSSSVSVSV"
 R_ENGINE = "VSVV"
-EW_ENGINE = "SSSS"
+EW_ENGINE = "VSSS"
 ORDER = (
     ("D", 5), ("NA", 0), ("NB", 0), ("R", 3), ("R", 1), ("T", 0), ("D", 1), ("R", 2),
     ("TW", 3), ("D", 1), ("E", 0), ("R", 0), ("TW", 2), ("EW", 3), ("Q", 0), ("TW", 1),
     ("D", 1), ("EW", 2), ("QW", 3), ("TW", 0), ("EW", 1), ("QW", 2), ("T", 1), ("EW", 0),
     ("QW", 1), ("QW", 0), ("E", 1), ("Q", 1), ("T", 2), ("D", 1), ("E", 2), ("Q", 2),
-    ("MA", 3), ("MA", 2), ("MA", 1), ("MA", 0), ("O", 0), ("M", 1), ("O", 1), ("T", 3),
-    ("E", 3), ("Q", 3), ("M", 2), ("O", 2), ("M", 3), ("O", 3), ("T", 4), ("E", 4),
-    ("Q", 4), ("T", 5), ("E", 5), ("Q", 5), ("M", 4), ("O", 4), ("M", 5), ("O", 5),
+    ("T", 3), ("E", 3), ("Q", 3), ("MA", 3), ("MA", 2), ("MA", 1), ("MA", 0), ("O", 0),
+    ("M", 1), ("O", 1), ("T", 4), ("E", 4), ("Q", 4), ("M", 2), ("O", 2), ("M", 3),
+    ("O", 3), ("T", 5), ("E", 5), ("Q", 5), ("M", 4), ("O", 4), ("M", 5), ("O", 5),
     ("T", 6), ("E", 6), ("Q", 6), ("M", 6), ("O", 6), ("M", 7), ("O", 7), ("T", 7),
     ("E", 7), ("Q", 7), ("M", 8), ("O", 8), ("M", 9), ("O", 9), ("T", 8), ("E", 8),
     ("Q", 8), ("M", 10), ("O", 10), ("M", 11), ("O", 11), ("T", 9), ("E", 9), ("Q", 9),

@@ -26,7 +26,7 @@ O_ENGINE = "SSSSSSSSSSSSSVSVSV"
 R_ENGINE = "VSVV"
 EW_ENGINE = "VSSS"
 ORDER = (
-    ("D", 5), ("NA", 0), ("NB", 0), ("R", 3), ("R", 1), ("T", 0), ("D", 1), ("R", 2),
+    ("D", 6), ("NA", 0), ("NB", 0), ("R", 3), ("R", 1), ("T", 0), ("D", 1), ("R", 2),
     ("TW", 3), ("D", 1), ("E", 0), ("R", 0), ("TW", 2), ("EW", 3), ("Q", 0), ("TW", 1),
     ("D", 1), ("EW", 2), ("QW", 3), ("TW", 0), ("EW", 1), ("QW", 2), ("T", 1), ("EW", 0),
     ("QW", 1), ("QW", 0), ("E", 1), ("Q", 1), ("T", 2), ("D", 1), ("E", 2), ("Q", 2),
@@ -61,6 +61,9 @@ def tile_quaternionlinear_kernel(tc, q_in, r_weight, i_weight, j_weight, k_weigh
         if PINNED:
             ctx.enter_context(tc.manual_schedule())
 
+        warm_src = keep.tile([P, P], F32, name="warm_src")
+        nc.vector.memset(warm_src[:], 0.0)
+
         planes = keep.tile([P, 9, P], BF16, name="planes")
         nc.sync.dma_start(out=planes[:, 0:9:8, :], in_=i_weight.unsqueeze(1).to_broadcast([P, 2, P]))
         nc.sync.dma_start(out=planes[:, 2, :], in_=k_weight)
@@ -87,13 +90,12 @@ def tile_quaternionlinear_kernel(tc, q_in, r_weight, i_weight, j_weight, k_weigh
         w_grouped = {}
 
         def plane_grid(d):
-            if d == 1:
-                return planes[:, 0:4, :].rearrange("p (b e) n -> p n b e", e=2)
-            if d == 2:
-                return planes[:, 5:9, :].rearrange("p (b e) n -> p n b e", e=2)
+            if d == 1 or d == 2:
+                base = 0 if d == 1 else 5
+                return planes[:, base : base + 4, :].rearrange("p (b e) (c i) -> p c b e i", e=2, i=4)
             base = 1 if d == 0 else 2
             six = planes[:, base : base + 6, :].rearrange("p (e x) n -> p e x n", x=3)
-            return six[:, :, 0:3:2, :].rearrange("p e b n -> p n b e")
+            return six[:, :, 0:3:2, :].rearrange("p e b (c i) -> p c b e i", i=4)
 
         def negate_ik():
             nc.vector.tensor_scalar_mul(out=planes[:, 4:7:2, :], in0=planes[:, 0:3:2, :], scalar1=-1.0)
@@ -102,7 +104,7 @@ def tile_quaternionlinear_kernel(tc, q_in, r_weight, i_weight, j_weight, k_weigh
             nc.gpsimd.tensor_scalar(out=planes[:, 3, :], in0=planes[:, 5, :], scalar1=-1.0, scalar2=0.0, op0=MULT, op1=ADD)
 
         def regroup(d):
-            copy(R_ENGINE[d], signed[:, d, :, :].rearrange("p n (b e) -> p n b e", e=2), plane_grid(d))
+            copy(R_ENGINE[d], signed[:, d, :, :].rearrange("p (c i) (b e) -> p c b e i", i=4, e=2), plane_grid(d))
 
         def w_transpose(d):
             tw = psum_o.tile([P, 2, P], F32, tag="o", name="tw%d" % d)
@@ -169,7 +171,7 @@ def tile_quaternionlinear_kernel(tc, q_in, r_weight, i_weight, j_weight, k_weigh
 
         def warm(n):
             for r in range(n):
-                nc.tensor.matmul(out=warm_bank[:], lhsT=ident[:], rhs=ident[:], start=True, stop=True)
+                nc.tensor.matmul(out=warm_bank[:], lhsT=warm_src[:], rhs=warm_src[:], start=True, stop=True)
 
 
         def multiply(t):

@@ -26,18 +26,17 @@ O_ENGINE = "SSSSSSSSSSSSSVSVSV"
 R_ENGINE = "VSVV"
 EW_ENGINE = "VSSS"
 ORDER = (
-    ("D", 6), ("NA", 0), ("NB", 0), ("R", 3), ("R", 1), ("T", 0), ("D", 1), ("R", 2),
-    ("TW", 3), ("D", 1), ("E", 0), ("R", 0), ("TW", 2), ("EW", 3), ("Q", 0), ("TW", 1),
-    ("D", 1), ("EW", 2), ("QW", 3), ("TW", 0), ("EW", 1), ("QW", 2), ("T", 1), ("EW", 0),
-    ("QW", 1), ("QW", 0), ("E", 1), ("Q", 1), ("T", 2), ("D", 1), ("E", 2), ("Q", 2),
-    ("T", 3), ("E", 3), ("Q", 3), ("MA", 3), ("MA", 2), ("MA", 1), ("MA", 0), ("O", 0),
-    ("M", 1), ("O", 1), ("T", 4), ("E", 4), ("Q", 4), ("M", 2), ("O", 2), ("M", 3),
-    ("O", 3), ("T", 5), ("E", 5), ("Q", 5), ("M", 4), ("O", 4), ("M", 5), ("O", 5),
-    ("T", 6), ("E", 6), ("Q", 6), ("M", 6), ("O", 6), ("M", 7), ("O", 7), ("T", 7),
-    ("E", 7), ("Q", 7), ("M", 8), ("O", 8), ("M", 9), ("O", 9), ("T", 8), ("E", 8),
-    ("Q", 8), ("M", 10), ("O", 10), ("M", 11), ("O", 11), ("T", 9), ("E", 9), ("Q", 9),
-    ("M", 12), ("O", 12), ("M", 13), ("O", 13), ("M", 14), ("O", 14), ("M", 15), ("O", 15),
-    ("M", 16), ("O", 16), ("M", 17), ("O", 17),
+    ("NA", 0), ("NB", 0), ("R", 3), ("R", 1), ("T", 0), ("R", 2), ("TW", 3), ("E", 0),
+    ("R", 0), ("TW", 2), ("EW", 3), ("Q", 0), ("TW", 1), ("EW", 2), ("QW", 3), ("TW", 0),
+    ("EW", 1), ("QW", 2), ("T", 1), ("EW", 0), ("QW", 1), ("QW", 0), ("E", 1), ("Q", 1),
+    ("T", 2), ("E", 2), ("Q", 2), ("T", 3), ("E", 3), ("Q", 3), ("MA", 3), ("MA", 2),
+    ("MA", 1), ("MA", 0), ("O", 0), ("M", 1), ("O", 1), ("T", 4), ("E", 4), ("Q", 4),
+    ("M", 2), ("O", 2), ("M", 3), ("O", 3), ("T", 5), ("E", 5), ("Q", 5), ("M", 4),
+    ("O", 4), ("M", 5), ("O", 5), ("T", 6), ("E", 6), ("Q", 6), ("M", 6), ("O", 6),
+    ("M", 7), ("O", 7), ("T", 7), ("E", 7), ("Q", 7), ("M", 8), ("O", 8), ("M", 9),
+    ("O", 9), ("T", 8), ("E", 8), ("Q", 8), ("M", 10), ("O", 10), ("M", 11), ("O", 11),
+    ("T", 9), ("E", 9), ("Q", 9), ("M", 12), ("O", 12), ("M", 13), ("O", 13), ("M", 14),
+    ("O", 14), ("M", 15), ("O", 15), ("M", 16), ("O", 16), ("M", 17), ("O", 17),
 )
 PINNED = True
 
@@ -56,13 +55,9 @@ def tile_quaternionlinear_kernel(tc, q_in, r_weight, i_weight, j_weight, k_weigh
     with ExitStack() as ctx:
         keep = ctx.enter_context(tc.tile_pool(name="keep", bufs=1))
         psum_t = ctx.enter_context(tc.psum_pool(name="psum_t", bufs=2))
-        psum_w = ctx.enter_context(tc.psum_pool(name="psum_w", bufs=1))
         psum_o = ctx.enter_context(tc.psum_pool(name="psum_o", bufs=5))
         if PINNED:
             ctx.enter_context(tc.manual_schedule())
-
-        warm_src = keep.tile([P, P], F32, name="warm_src")
-        nc.vector.memset(warm_src[:], 0.0)
 
         planes = keep.tile([P, 9, P], BF16, name="planes")
         nc.sync.dma_start(out=planes[:, 0:9:8, :], in_=i_weight.unsqueeze(1).to_broadcast([P, 2, P]))
@@ -167,12 +162,6 @@ def tile_quaternionlinear_kernel(tc, q_in, r_weight, i_weight, j_weight, k_weigh
                 store_of[t] = (si, s)
 
         accs = {}
-        warm_bank = psum_w.tile([P, P], F32, name="warm_bank")
-
-        def warm(n):
-            for r in range(n):
-                nc.tensor.matmul(out=warm_bank[:], lhsT=warm_src[:], rhs=warm_src[:], start=True, stop=True)
-
 
         def multiply(t):
             g, s = slot_of[t]
@@ -230,7 +219,6 @@ def tile_quaternionlinear_kernel(tc, q_in, r_weight, i_weight, j_weight, k_weigh
             "M": multiply,
             "MA": multiply_component,
             "O": o_evacuate,
-            "D": warm,
         }
         for name, index in ORDER:
             actions[name](index)

@@ -19,26 +19,9 @@ TILES = TOKENS // P
 FLOPS = 2 * TOKENS * K * N_OUT
 
 LOAD_CHUNKS = (1, 3, 4, 4, 6)
-GROUPS = ((0,), (1,), (2, 3), (4, 5), (6, 7), (8, 9), (10, 11), (12, 13), (14, 15), (16, 17))
-STORES = ((0,), (1,), (2, 3), (4, 5), (6, 7), (8, 9), (10, 11), (12, 13), (14, 15), (16,), (17,))
-E_ENGINE = "SSSVVVVVVV"
-O_ENGINE = "SSSSSSSSSSSSSVSVSV"
-R_ENGINE = "VSVV"
-EW_ENGINE = "VSSS"
-ORDER = (
-    ("NA", 0), ("NB", 0), ("R", 3), ("R", 1), ("T", 0), ("R", 2), ("TW", 3), ("E", 0),
-    ("R", 0), ("TW", 2), ("EW", 3), ("Q", 0), ("TW", 1), ("EW", 2), ("QW", 3), ("TW", 0),
-    ("EW", 1), ("QW", 2), ("T", 1), ("EW", 0), ("QW", 1), ("QW", 0), ("E", 1), ("Q", 1),
-    ("T", 2), ("E", 2), ("Q", 2), ("T", 3), ("E", 3), ("Q", 3), ("MA", 3), ("MA", 2),
-    ("MA", 1), ("MA", 0), ("O", 0), ("M", 1), ("O", 1), ("T", 4), ("E", 4), ("Q", 4),
-    ("M", 2), ("O", 2), ("M", 3), ("O", 3), ("T", 5), ("E", 5), ("Q", 5), ("M", 4),
-    ("O", 4), ("M", 5), ("O", 5), ("T", 6), ("E", 6), ("Q", 6), ("M", 6), ("O", 6),
-    ("M", 7), ("O", 7), ("T", 7), ("E", 7), ("Q", 7), ("M", 8), ("O", 8), ("M", 9),
-    ("O", 9), ("T", 8), ("E", 8), ("Q", 8), ("M", 10), ("O", 10), ("M", 11), ("O", 11),
-    ("T", 9), ("E", 9), ("Q", 9), ("M", 12), ("O", 12), ("M", 13), ("O", 13), ("M", 14),
-    ("O", 14), ("M", 15), ("O", 15), ("M", 16), ("O", 16), ("M", 17), ("O", 17),
-)
-PINNED = True
+GROUPS = ((0,), (1,)) + tuple((t, t + 1) for t in range(2, TILES, 2))
+STORES = ((0,), (1,)) + tuple((t, t + 1) for t in range(2, TILES - 2, 2)) + ((TILES - 2,), (TILES - 1,))
+LEAD = 2
 
 
 def tile_quaternionlinear_kernel(tc, q_in, r_weight, i_weight, j_weight, k_weight, out):
@@ -55,9 +38,9 @@ def tile_quaternionlinear_kernel(tc, q_in, r_weight, i_weight, j_weight, k_weigh
     with ExitStack() as ctx:
         keep = ctx.enter_context(tc.tile_pool(name="keep", bufs=1))
         psum_t = ctx.enter_context(tc.psum_pool(name="psum_t", bufs=2))
+        psum_w = ctx.enter_context(tc.psum_pool(name="psum_w", bufs=1))
         psum_o = ctx.enter_context(tc.psum_pool(name="psum_o", bufs=5))
-        if PINNED:
-            ctx.enter_context(tc.manual_schedule())
+        ctx.enter_context(tc.manual_schedule())
 
         planes = keep.tile([P, 9, P], BF16, name="planes")
         nc.sync.dma_start(out=planes[:, 0:9:8, :], in_=i_weight.unsqueeze(1).to_broadcast([P, 2, P]))
@@ -85,35 +68,38 @@ def tile_quaternionlinear_kernel(tc, q_in, r_weight, i_weight, j_weight, k_weigh
         w_grouped = {}
 
         def plane_grid(d):
-            if d == 1 or d == 2:
-                base = 0 if d == 1 else 5
-                return planes[:, base : base + 4, :].rearrange("p (b e) (c i) -> p c b e i", e=2, i=4)
+            if d == 1:
+                return planes[:, 0:4, :].rearrange("p (b e) n -> p n b e", e=2)
+            if d == 2:
+                return planes[:, 5:9, :].rearrange("p (b e) n -> p n b e", e=2)
             base = 1 if d == 0 else 2
             six = planes[:, base : base + 6, :].rearrange("p (e x) n -> p e x n", x=3)
-            return six[:, :, 0:3:2, :].rearrange("p e b (c i) -> p c b e i", i=4)
+            return six[:, :, 0:3:2, :].rearrange("p e b n -> p n b e")
 
-        def negate_ik():
+        def negate_i_and_k():
             nc.vector.tensor_scalar_mul(out=planes[:, 4:7:2, :], in0=planes[:, 0:3:2, :], scalar1=-1.0)
 
         def negate_j():
             nc.gpsimd.tensor_scalar(out=planes[:, 3, :], in0=planes[:, 5, :], scalar1=-1.0, scalar2=0.0, op0=MULT, op1=ADD)
 
         def regroup(d):
-            copy(R_ENGINE[d], signed[:, d, :, :].rearrange("p (c i) (b e) -> p c b e i", i=4, e=2), plane_grid(d))
+            engine = "S" if d == 1 else "V"
+            copy(engine, signed[:, d, :, :].rearrange("p n (b e) -> p n b e", e=2), plane_grid(d))
 
-        def w_transpose(d):
+        def transpose_weights(d):
             tw = psum_o.tile([P, 2, P], F32, tag="o", name="tw%d" % d)
             for u in range(2):
                 col = (2 * d + u) * P
                 nc.tensor.transpose(tw[:, u, :], signed_words[:, col : col + P], ident[:])
             w_banks[d] = tw
 
-        def w_evacuate(d):
+        def copy_weights(d):
             wg = keep.tile([P, 4 * P], BF16, name="w_grouped%d" % d, align_bytes=64)
-            copy(EW_ENGINE[d], wg[:].bitcast(F32).rearrange("p (m u) -> p m u", u=2), w_banks[d][:].rearrange("p u m -> p m u"))
+            engine = "V" if d == 0 else "S"
+            copy(engine, wg[:].bitcast(F32).rearrange("p (m u) -> p m u", u=2), w_banks[d][:].rearrange("p u m -> p m u"))
             w_grouped[d] = wg
 
-        def w_quantise(d):
+        def quantise_weights(d):
             cols = slice(d * P, (d + 1) * P)
             nc.vector.quantize_mx(out=w_codes[:, cols].bitcast(FP8X4), scales=w_scales[:, cols], in_=w_grouped[d][:])
 
@@ -126,7 +112,7 @@ def tile_quaternionlinear_kernel(tc, q_in, r_weight, i_weight, j_weight, k_weigh
             for s, t in enumerate(tiles):
                 slot_of[t] = (g, s)
 
-        def q_transpose(g):
+        def transpose_tokens(g):
             n = len(GROUPS[g])
             tq = psum_t.tile([P, n, 2, P], F32, tag="t", name="tq%d" % g)
             for s, t in enumerate(GROUPS[g]):
@@ -135,23 +121,28 @@ def tile_quaternionlinear_kernel(tc, q_in, r_weight, i_weight, j_weight, k_weigh
                     nc.tensor.transpose(tq[:, s, u, :], words[:, u * P : (u + 1) * P], ident[:])
             q_banks[g] = tq
 
-        def q_evacuate(g):
+        def copy_tokens(g):
             n = len(GROUPS[g])
             grouped = keep.tile([P, n * 4 * P], BF16, name="grouped%d" % g, align_bytes=64)
             copy(
-                E_ENGINE[g],
+                "S" if g < 3 else "V",
                 grouped[:].bitcast(F32).rearrange("p (s k u) -> p s k u", s=n, u=2),
                 q_banks[g][:].rearrange("p s u k -> p s k u"),
             )
             q_grouped[g] = grouped
 
-        def q_quantise(g):
+        def quantise_tokens(g):
             n = len(GROUPS[g])
             codes = keep.tile([P, n * P], U32, name="codes%d" % g, align_bytes=64)
             scales = keep.tile([P, n * P], U8, name="scales%d" % g, align_bytes=64)
             nc.vector.quantize_mx(out=codes[:].bitcast(FP8X4), scales=scales[:], in_=q_grouped[g][:])
             q_codes[g] = codes
             q_scales[g] = scales
+
+        def prepare(g):
+            transpose_tokens(g)
+            copy_tokens(g)
+            quantise_tokens(g)
 
         store_of = {}
         o_tiles = {}
@@ -162,6 +153,11 @@ def tile_quaternionlinear_kernel(tc, q_in, r_weight, i_weight, j_weight, k_weigh
                 store_of[t] = (si, s)
 
         accs = {}
+        warm_bank = psum_w.tile([P, P], F32, name="warm_bank")
+
+        def warm(n):
+            for r in range(n):
+                nc.tensor.matmul(out=warm_bank[:], lhsT=ident[:], rhs=ident[:], start=True, stop=True)
 
         def multiply(t):
             g, s = slot_of[t]
@@ -192,12 +188,12 @@ def tile_quaternionlinear_kernel(tc, q_in, r_weight, i_weight, j_weight, k_weigh
                 stop=True,
             )
 
-        def o_evacuate(t):
+        def copy_out(t):
             si, ss = store_of[t]
             if si not in o_tiles:
                 o_tiles[si] = keep.tile([P, len(STORES[si]), N_OUT], F32, name="o_sb%d" % si)
             copy(
-                O_ENGINE[t],
+                "V" if t >= TILES - 5 and t % 2 == 1 else "S",
                 o_tiles[si][:, ss, :].rearrange("p (m d) -> p m d", d=4),
                 accs[t][:].rearrange("p (d m) -> p m d", d=4),
             )
@@ -206,19 +202,47 @@ def tile_quaternionlinear_kernel(tc, q_in, r_weight, i_weight, j_weight, k_weigh
                 t0 = STORES[si][0]
                 nc.sync.dma_start(out=out_view[:, t0 : t0 + len(STORES[si]), :], in_=o_tiles[si][:])
 
-        actions = {
-            "NA": lambda x: negate_ik(),
-            "NB": lambda x: negate_j(),
-            "R": regroup,
-            "TW": w_transpose,
-            "EW": w_evacuate,
-            "QW": w_quantise,
-            "T": q_transpose,
-            "E": q_evacuate,
-            "Q": q_quantise,
-            "M": multiply,
-            "MA": multiply_component,
-            "O": o_evacuate,
-        }
-        for name, index in ORDER:
-            actions[name](index)
+        warm(5)
+        negate_i_and_k()
+        negate_j()
+        regroup(3)
+        regroup(1)
+        transpose_tokens(0)
+        warm(1)
+        regroup(2)
+        transpose_weights(3)
+        warm(1)
+        copy_tokens(0)
+        regroup(0)
+        transpose_weights(2)
+        copy_weights(3)
+        quantise_tokens(0)
+        transpose_weights(1)
+        copy_weights(2)
+        quantise_weights(3)
+        transpose_weights(0)
+        warm(1)
+        copy_weights(1)
+        quantise_weights(2)
+        transpose_tokens(1)
+        copy_weights(0)
+        quantise_weights(1)
+        quantise_weights(0)
+        copy_tokens(1)
+        quantise_tokens(1)
+        transpose_tokens(2)
+        warm(1)
+        copy_tokens(2)
+        quantise_tokens(2)
+        prepare(3)
+        for d in (3, 2, 1, 0):
+            multiply_component(d)
+        copy_out(0)
+        multiply(1)
+        copy_out(1)
+        for g in range(2, len(GROUPS)):
+            if g + LEAD < len(GROUPS):
+                prepare(g + LEAD)
+            for t in GROUPS[g]:
+                multiply(t)
+                copy_out(t)

@@ -50,12 +50,12 @@ def tile_quaternionlinear_kernel(tc, q_in, r_weight, i_weight, j_weight, k_weigh
 
         q_tiles = []
         first = 0
-        for ci, n in enumerate(LOAD_CHUNKS):
-            q_chunk = keep.tile([P, n, K], BF16, name="q_chunk%d" % ci)
-            nc.sync.dma_start(out=q_chunk[:], in_=q_view[:, first : first + n, :])
-            for j in range(n):
+        for ci, count in enumerate(LOAD_CHUNKS):
+            q_chunk = keep.tile([P, count, K], BF16, name="q_chunk%d" % ci)
+            nc.sync.dma_start(out=q_chunk[:], in_=q_view[:, first : first + count, :])
+            for j in range(count):
                 q_tiles.append(q_chunk[:, j, :])
-            first += n
+            first += count
 
         ident = keep.tile([P, P], F32, name="ident")
         make_identity(nc, ident[:])
@@ -113,8 +113,8 @@ def tile_quaternionlinear_kernel(tc, q_in, r_weight, i_weight, j_weight, k_weigh
                 slot_of[t] = (g, s)
 
         def transpose_tokens(g):
-            n = len(GROUPS[g])
-            tq = psum_t.tile([P, n, 2, P], F32, tag="t", name="tq%d" % g)
+            count = len(GROUPS[g])
+            tq = psum_t.tile([P, count, 2, P], F32, tag="t", name="tq%d" % g)
             for s, t in enumerate(GROUPS[g]):
                 words = q_tiles[t].bitcast(F32)
                 for u in range(2):
@@ -122,19 +122,19 @@ def tile_quaternionlinear_kernel(tc, q_in, r_weight, i_weight, j_weight, k_weigh
             q_banks[g] = tq
 
         def copy_tokens(g):
-            n = len(GROUPS[g])
-            grouped = keep.tile([P, n * 4 * P], BF16, name="grouped%d" % g, align_bytes=64)
+            count = len(GROUPS[g])
+            grouped = keep.tile([P, count * 4 * P], BF16, name="grouped%d" % g, align_bytes=64)
             copy(
                 "S" if g < 3 else "V",
-                grouped[:].bitcast(F32).rearrange("p (s k u) -> p s k u", s=n, u=2),
+                grouped[:].bitcast(F32).rearrange("p (s k u) -> p s k u", s=count, u=2),
                 q_banks[g][:].rearrange("p s u k -> p s k u"),
             )
             q_grouped[g] = grouped
 
         def quantise_tokens(g):
-            n = len(GROUPS[g])
-            codes = keep.tile([P, n * P], U32, name="codes%d" % g, align_bytes=64)
-            scales = keep.tile([P, n * P], U8, name="scales%d" % g, align_bytes=64)
+            count = len(GROUPS[g])
+            codes = keep.tile([P, count * P], U32, name="codes%d" % g, align_bytes=64)
+            scales = keep.tile([P, count * P], U8, name="scales%d" % g, align_bytes=64)
             nc.vector.quantize_mx(out=codes[:].bitcast(FP8X4), scales=scales[:], in_=q_grouped[g][:])
             q_codes[g] = codes
             q_scales[g] = scales
@@ -145,7 +145,7 @@ def tile_quaternionlinear_kernel(tc, q_in, r_weight, i_weight, j_weight, k_weigh
             quantise_tokens(g)
 
         store_of = {}
-        o_tiles = {}
+        store_rows = {}
         left = {}
         for si, tiles in enumerate(STORES):
             left[si] = len(tiles)
@@ -155,8 +155,8 @@ def tile_quaternionlinear_kernel(tc, q_in, r_weight, i_weight, j_weight, k_weigh
         accs = {}
         warm_bank = psum_w.tile([P, P], F32, name="warm_bank")
 
-        def warm(n):
-            for r in range(n):
+        def warm(count):
+            for r in range(count):
                 nc.tensor.matmul(out=warm_bank[:], lhsT=ident[:], rhs=ident[:], start=True, stop=True)
 
         def multiply(t):
@@ -190,17 +190,17 @@ def tile_quaternionlinear_kernel(tc, q_in, r_weight, i_weight, j_weight, k_weigh
 
         def copy_out(t):
             si, ss = store_of[t]
-            if si not in o_tiles:
-                o_tiles[si] = keep.tile([P, len(STORES[si]), N_OUT], F32, name="o_sb%d" % si)
+            if si not in store_rows:
+                store_rows[si] = keep.tile([P, len(STORES[si]), N_OUT], F32, name="o_sb%d" % si)
             copy(
                 "V" if t >= TILES - 5 and t % 2 == 1 else "S",
-                o_tiles[si][:, ss, :].rearrange("p (m d) -> p m d", d=4),
+                store_rows[si][:, ss, :].rearrange("p (m d) -> p m d", d=4),
                 accs[t][:].rearrange("p (d m) -> p m d", d=4),
             )
             left[si] -= 1
             if left[si] == 0:
                 t0 = STORES[si][0]
-                nc.sync.dma_start(out=out_view[:, t0 : t0 + len(STORES[si]), :], in_=o_tiles[si][:])
+                nc.sync.dma_start(out=out_view[:, t0 : t0 + len(STORES[si]), :], in_=store_rows[si][:])
 
         warm(5)
         negate_i_and_k()
@@ -218,10 +218,10 @@ def tile_quaternionlinear_kernel(tc, q_in, r_weight, i_weight, j_weight, k_weigh
         copy_weights(3)
         quantise_tokens(0)
         transpose_weights(1)
+        warm(1)
         copy_weights(2)
         quantise_weights(3)
         transpose_weights(0)
-        warm(1)
         copy_weights(1)
         quantise_weights(2)
         transpose_tokens(1)
@@ -240,9 +240,10 @@ def tile_quaternionlinear_kernel(tc, q_in, r_weight, i_weight, j_weight, k_weigh
         copy_out(0)
         multiply(1)
         copy_out(1)
-        for g in range(2, len(GROUPS)):
-            if g + LEAD < len(GROUPS):
-                prepare(g + LEAD)
-            for t in GROUPS[g]:
+        for g in range(2, len(GROUPS), 2):
+            for h in (g + LEAD, g + LEAD + 1):
+                if h < len(GROUPS):
+                    prepare(h)
+            for t in GROUPS[g] + GROUPS[g + 1]:
                 multiply(t)
                 copy_out(t)

from contextlib import ExitStack

import concourse.mybir as mybir
from concourse.masks import make_identity

F32 = mybir.dt.float32
BF16 = mybir.dt.bfloat16
U32 = mybir.dt.uint32
U8 = mybir.dt.uint8
FP8X4 = mybir.dt.float8_e4m3fn_x4
MULT = mybir.AluOpType.mult
ADD = mybir.AluOpType.add

P = 128
TOKENS = 4 * 576
K = 512
N_OUT = 512
TILES = TOKENS // P
FLOPS = 2 * TOKENS * K * N_OUT

LOAD_CHUNKS = (1, 3, 4, 4, 6)
GROUPS = ((0,), (1,)) + tuple((t, t + 1) for t in range(2, TILES, 2))
STORES = ((0,), (1,)) + tuple((t, t + 1) for t in range(2, TILES - 2, 2)) + ((TILES - 2,), (TILES - 1,))
LEAD = 2


def tile_quaternionlinear_kernel(tc, q_in, r_weight, i_weight, j_weight, k_weight, out):
    nc = tc.nc
    q_view = q_in.flatten_outer_dims().rearrange("(p t) k -> p t k", t=TILES)
    out_view = out.flatten_outer_dims().rearrange("(p t) c -> p t c", t=TILES)

    def copy(engine, dst, src):
        if engine == "V":
            nc.vector.tensor_copy(out=dst, in_=src)
        else:
            nc.scalar.copy(out=dst, in_=src)

    with ExitStack() as ctx:
        keep = ctx.enter_context(tc.tile_pool(name="keep", bufs=1))
        psum_t = ctx.enter_context(tc.psum_pool(name="psum_t", bufs=2))
        psum_w = ctx.enter_context(tc.psum_pool(name="psum_w", bufs=1))
        psum_o = ctx.enter_context(tc.psum_pool(name="psum_o", bufs=5))
        ctx.enter_context(tc.manual_schedule())

        planes = keep.tile([P, 9, P], BF16, name="planes")
        nc.sync.dma_start(out=planes[:, 0:9:8, :], in_=i_weight.unsqueeze(1).to_broadcast([P, 2, P]))
        nc.sync.dma_start(out=planes[:, 2, :], in_=k_weight)
        nc.sync.dma_start(out=planes[:, 5, :], in_=j_weight)
        nc.sync.dma_start(out=planes[:, 1:8:6, :], in_=r_weight.unsqueeze(1).to_broadcast([P, 2, P]))

        q_tiles = []
        first = 0
        for ci, count in enumerate(LOAD_CHUNKS):
            q_chunk = keep.tile([P, count, K], BF16, name="q_chunk%d" % ci)
            nc.sync.dma_start(out=q_chunk[:], in_=q_view[:, first : first + count, :])
            for j in range(count):
                q_tiles.append(q_chunk[:, j, :])
            first += count

        ident = keep.tile([P, P], F32, name="ident")
        make_identity(nc, ident[:])

        signed = keep.tile([P, 4, P, 4], BF16, name="signed")
        signed_words = signed[:].rearrange("p d n c -> p (d n c)").bitcast(F32)
        w_codes = keep.tile([P, N_OUT], U32, name="w_codes", align_bytes=64)
        w_scales = keep.tile([P, N_OUT], U8, name="w_scales", align_bytes=64)
        w_banks = {}
        w_grouped = {}

        def plane_grid(d):
            if d == 1:
                return planes[:, 0:4, :].rearrange("p (b e) n -> p n b e", e=2)
            if d == 2:
                return planes[:, 5:9, :].rearrange("p (b e) n -> p n b e", e=2)
            base = 1 if d == 0 else 2
            six = planes[:, base : base + 6, :].rearrange("p (e x) n -> p e x n", x=3)
            return six[:, :, 0:3:2, :].rearrange("p e b n -> p n b e")

        def negate_i_and_k():
            nc.vector.tensor_scalar_mul(out=planes[:, 4:7:2, :], in0=planes[:, 0:3:2, :], scalar1=-1.0)

        def negate_j():
            nc.gpsimd.tensor_scalar(out=planes[:, 3, :], in0=planes[:, 5, :], scalar1=-1.0, scalar2=0.0, op0=MULT, op1=ADD)

        def regroup(d):
            engine = "S" if d == 1 else "V"
            copy(engine, signed[:, d, :, :].rearrange("p n (b e) -> p n b e", e=2), plane_grid(d))

        def transpose_weights(d):
            tw = psum_o.tile([P, 2, P], F32, tag="o", name="tw%d" % d)
            for u in range(2):
                col = (2 * d + u) * P
                nc.tensor.transpose(tw[:, u, :], signed_words[:, col : col + P], ident[:])
            w_banks[d] = tw

        def copy_weights(d):
            wg = keep.tile([P, 4 * P], BF16, name="w_grouped%d" % d, align_bytes=64)
            engine = "V" if d == 0 else "S"
            copy(engine, wg[:].bitcast(F32).rearrange("p (m u) -> p m u", u=2), w_banks[d][:].rearrange("p u m -> p m u"))
            w_grouped[d] = wg

        def quantise_weights(d):
            cols = slice(d * P, (d + 1) * P)
            nc.vector.quantize_mx(out=w_codes[:, cols].bitcast(FP8X4), scales=w_scales[:, cols], in_=w_grouped[d][:])

        q_banks = {}
        q_grouped = {}
        q_codes = {}
        q_scales = {}
        slot_of = {}
        for g, tiles in enumerate(GROUPS):
            for s, t in enumerate(tiles):
                slot_of[t] = (g, s)

        def transpose_tokens(g):
            count = len(GROUPS[g])
            tq = psum_t.tile([P, count, 2, P], F32, tag="t", name="tq%d" % g)
            for s, t in enumerate(GROUPS[g]):
                words = q_tiles[t].bitcast(F32)
                for u in range(2):
                    nc.tensor.transpose(tq[:, s, u, :], words[:, u * P : (u + 1) * P], ident[:])
            q_banks[g] = tq

        def copy_tokens(g):
            count = len(GROUPS[g])
            grouped = keep.tile([P, count * 4 * P], BF16, name="grouped%d" % g, align_bytes=64)
            copy(
                "S" if g < 3 else "V",
                grouped[:].bitcast(F32).rearrange("p (s k u) -> p s k u", s=count, u=2),
                q_banks[g][:].rearrange("p s u k -> p s k u"),
            )
            q_grouped[g] = grouped

        def quantise_tokens(g):
            count = len(GROUPS[g])
            codes = keep.tile([P, count * P], U32, name="codes%d" % g, align_bytes=64)
            scales = keep.tile([P, count * P], U8, name="scales%d" % g, align_bytes=64)
            nc.vector.quantize_mx(out=codes[:].bitcast(FP8X4), scales=scales[:], in_=q_grouped[g][:])
            q_codes[g] = codes
            q_scales[g] = scales

        def prepare(g):
            transpose_tokens(g)
            copy_tokens(g)
            quantise_tokens(g)

        store_of = {}
        store_rows = {}
        left = {}
        for si, tiles in enumerate(STORES):
            left[si] = len(tiles)
            for s, t in enumerate(tiles):
                store_of[t] = (si, s)

        accs = {}
        warm_bank = psum_w.tile([P, P], F32, name="warm_bank")

        def warm(count):
            for r in range(count):
                nc.tensor.matmul(out=warm_bank[:], lhsT=ident[:], rhs=ident[:], start=True, stop=True)

        def multiply(t):
            g, s = slot_of[t]
            acc = psum_o.tile([P, N_OUT], F32, tag="o", name="acc%d" % t)
            nc.tensor.matmul_mx(
                out=acc[:],
                lhsT=q_codes[g][:, s * P : (s + 1) * P].bitcast(FP8X4),
                lhsT_scale=q_scales[g][:, s * P : (s + 1) * P],
                rhs=w_codes[:].bitcast(FP8X4),
                rhs_scale=w_scales[:],
                start=True,
                stop=True,
            )
            accs[t] = acc

        def multiply_component(d):
            g, s = slot_of[0]
            if 0 not in accs:
                accs[0] = psum_o.tile([P, N_OUT], F32, tag="o", name="acc0")
            cols = slice(d * P, (d + 1) * P)
            nc.tensor.matmul_mx(
                out=accs[0][:, cols],
                lhsT=q_codes[g][:, s * P : (s + 1) * P].bitcast(FP8X4),
                lhsT_scale=q_scales[g][:, s * P : (s + 1) * P],
                rhs=w_codes[:, cols].bitcast(FP8X4),
                rhs_scale=w_scales[:, cols],
                start=True,
                stop=True,
            )

        def copy_out(t):
            si, ss = store_of[t]
            if si not in store_rows:
                store_rows[si] = keep.tile([P, len(STORES[si]), N_OUT], F32, name="o_sb%d" % si)
            copy(
                "V" if t >= TILES - 5 and t % 2 == 1 else "S",
                store_rows[si][:, ss, :].rearrange("p (m d) -> p m d", d=4),
                accs[t][:].rearrange("p (d m) -> p m d", d=4),
            )
            left[si] -= 1
            if left[si] == 0:
                t0 = STORES[si][0]
                nc.sync.dma_start(out=out_view[:, t0 : t0 + len(STORES[si]), :], in_=store_rows[si][:])

        warm(5)
        negate_i_and_k()
        negate_j()
        regroup(3)
        regroup(1)
        transpose_tokens(0)
        warm(1)
        regroup(2)
        transpose_weights(3)
        warm(1)
        copy_tokens(0)
        regroup(0)
        transpose_weights(2)
        copy_weights(3)
        quantise_tokens(0)
        transpose_weights(1)
        warm(1)
        copy_weights(2)
        quantise_weights(3)
        transpose_weights(0)
        copy_weights(1)
        quantise_weights(2)
        transpose_tokens(1)
        copy_weights(0)
        quantise_weights(1)
        quantise_weights(0)
        copy_tokens(1)
        quantise_tokens(1)
        transpose_tokens(2)
        warm(1)
        copy_tokens(2)
        quantise_tokens(2)
        prepare(3)
        for d in (3, 2, 1, 0):
            multiply_component(d)
        copy_out(0)
        multiply(1)
        copy_out(1)
        for g in range(2, len(GROUPS), 2):
            for h in (g + LEAD, g + LEAD + 1):
                if h < len(GROUPS):
                    prepare(h)
            for t in GROUPS[g] + GROUPS[g + 1]:
                multiply(t)
                copy_out(t)
